import numpy as np
import ml_dtypes


def mxq(x, axis, fmt="e4m3"):
    dtype, down = {"e4m3": (ml_dtypes.float8_e4m3fn, 7), "e5m2": (ml_dtypes.float8_e5m2, 14)}[fmt]
    v = np.moveaxis(np.asarray(x, np.float32).astype(ml_dtypes.bfloat16).astype(np.float64), axis, -1)
    blocks = v.reshape(v.shape[:-1] + (-1, 32))
    amax = np.abs(blocks).max(-1, keepdims=True)
    byte = np.maximum(np.where(amax > 0, np.frexp(amax)[1] - 1 + 127, 0) - down, 1)
    scale = np.exp2(byte - 127.0)
    codes = (blocks / scale).astype(np.float32).astype(dtype).astype(np.float64)
    return np.moveaxis((codes * scale).reshape(v.shape), -1, axis)


WIDE = False


def mx_kscale(k):
    if not WIDE:
        return np.ones(k)
    levels = np.array([10, -10, 5, -5, 0])
    a = np.random.permutation(np.resize(levels, k // 512 * 4)).reshape(k // 512, 4)
    idx = np.arange(k)
    return np.exp2(a[idx // 512, idx % 128 // 32])


BF16 = ml_dtypes.bfloat16


def bf(x):
    return np.asarray(x, np.float32).astype(BF16)


def f64(x):
    return np.asarray(x).astype(np.float64)


E2M1 = np.array([0.0, 0.5, 1.0, 1.5, 2.0, 3.0, 4.0, 6.0, -0.0, -0.5, -1.0, -1.5, -2.0, -3.0, -4.0, -6.0])


def pack_weight(w, fmt):
    k, n = w.shape
    w = f64(bf(w)).reshape(k // 32, 32, n)
    amax = np.abs(w).max(1)
    if fmt == "e4m3":
        byte = np.frexp(amax)[1] - 1 + 127 - 7
    else:
        mant, ex = np.frexp(amax / 6.0)
        byte = np.where(mant > 0.5, ex, ex - 1) + 127
    byte = np.clip(np.where(amax > 0, byte, 1), 1, 254)
    scaled = (w * np.exp2(127.0 - byte)[:, None, :]).reshape(k, n).astype(np.float32)
    by_word = np.ascontiguousarray(scaled.reshape(k // 512, 128, 4, n).transpose(0, 1, 3, 2))
    if fmt == "e4m3":
        words = by_word.astype(ml_dtypes.float8_e4m3fn).view(np.uint8)
    else:
        c = by_word.astype(ml_dtypes.float4_e2m1fn).view(np.uint8) & 0xF
        words = c[..., 0::2] | (c[..., 1::2] << 4)
    return np.ascontiguousarray(words), np.ascontiguousarray(byte.astype(np.uint8).reshape(k // 512, 16, n))


def unpack_weight(words, scales, fmt):
    g, p, n, _ = words.shape
    if fmt == "e4m3":
        vals = np.ascontiguousarray(words).view(ml_dtypes.float8_e4m3fn).astype(np.float64)
    else:
        nib = np.empty((g, p, n, 4), np.uint8)
        nib[..., 0::2] = words & 0xF
        nib[..., 1::2] = words >> 4
        vals = E2M1[nib]
    vals = vals * np.repeat(np.exp2(scales.astype(np.float64) - 127.0), 8, axis=1)[..., None]
    return vals.transpose(0, 1, 3, 2).reshape(g * 512, n)


B, S, IN_DIM, OUT_DIM, MOD_DIM = 4, 512, 512, 512, 512
EPS = 1e-8
GAIN = np.sqrt(2.0 / (1.0 + 0.2 ** 2))


def setup_inputs():
    ks = mx_kscale(MOD_DIM)
    kt = mx_kscale(IN_DIM)
    x = bf(np.random.standard_normal((B, S, IN_DIM)))
    modulation = bf(np.random.standard_normal((B, S, MOD_DIM)) * ks)
    weight = bf(np.random.standard_normal((OUT_DIM, IN_DIM)) * GAIN / np.sqrt(IN_DIM) / kt[None, :])
    bias = bf(np.random.standard_normal(OUT_DIM) * 0.1)
    mod_w = np.random.standard_normal((IN_DIM, MOD_DIM)) / np.sqrt(MOD_DIM) * kt[:, None] / ks[None, :]
    mod_w_words, mod_w_scales = pack_weight(np.ascontiguousarray(mod_w.T), "e4m3")
    mod_b = bf((1.0 + 0.1 * np.random.standard_normal(IN_DIM)) * kt)
    return {"x": x,
            "modulation": modulation,
            "weight": weight,
            "bias": bias,
            "mod_w_words": mod_w_words,
            "mod_w_scales": mod_w_scales,
            "mod_b": mod_b}


def reference(x, modulation, weight, bias, mod_w_words, mod_w_scales, mod_b):
    xf, w = f64(x), f64(weight)
    s = (mxq(f64(modulation), 2, "e4m3") @ unpack_weight(mod_w_words, mod_w_scales, "e4m3")) + f64(mod_b)
    out = mxq(xf * s, 2, "e4m3") @ mxq(w, 1, "e4m3").T
    demod = 1.0 / np.sqrt((mxq(s * s, 2, "e4m3") @ mxq(w * w, 1, "e4m3").T) + EPS)
    return out * demod + f64(bias)

@@ -1,0 +1,255 @@
+from contextlib import ExitStack
+
+import concourse.mybir as mybir
+from concourse.masks import make_identity
+
+F32 = mybir.dt.float32
+BF16 = mybir.dt.bfloat16
+I32 = mybir.dt.int32
+U32 = mybir.dt.uint32
+U8 = mybir.dt.uint8
+FP8X4 = mybir.dt.float8_e4m3fn_x4
+ACT = mybir.ActivationFunctionType
+ALU = mybir.AluOpType
+
+P = 128
+PACK = 4
+K = P * PACK
+FEATURES = 512
+TOKENS = 4 * 512
+TILES = TOKENS // P
+UNIT_TILES = 2
+UNIT = UNIT_TILES * P
+UNITS = TILES // UNIT_TILES
+EPS = 1e-8
+WEIGHT_ROUND = 1
+
+FLOPS = 3 * 2 * TOKENS * K * FEATURES
+
+
+def tile_modulatedlinear_kernel(
+    tc, x, modulation, weight, bias, mod_w_words, mod_w_scales, mod_b, out
+):
+    nc = tc.nc
+    x_rows = x.flatten_outer_dims().rearrange("(p j) k -> p j k", j=TILES)
+    mod_rows = modulation.flatten_outer_dims().rearrange("(p j) k -> p j k", j=TILES)
+    out_rows = out.flatten_outer_dims().rearrange("(p j) n -> p j n", j=TILES)
+
+    with ExitStack() as ctx:
+        const = ctx.enter_context(tc.tile_pool(name="const", bufs=1))
+        loads = ctx.enter_context(tc.tile_pool(name="loads", bufs=1))
+        work = ctx.enter_context(tc.tile_pool(name="work", bufs=3))
+        psum = ctx.enter_context(tc.psum_pool(name="psum", bufs=2))
+
+        w1_scales = const.tile([P, FEATURES], U8, align_bytes=64)
+        nc.vector.memset(w1_scales[:].bitcast(I32), 0)
+        for quadrant in range(4):
+            nc.sync.dma_start(
+                out=w1_scales[32 * quadrant : 32 * quadrant + 4, :].bitcast(I32),
+                in_=mod_w_scales[0, 4 * quadrant : 4 * quadrant + 4, :].bitcast(I32),
+            )
+        w1_codes = const.tile([P, FEATURES], U32, align_bytes=64)
+        nc.sync.dma_start(
+            out=w1_codes[:].bitcast(I32),
+            in_=mod_w_words[0].rearrange("p n t -> p (n t)").bitcast(I32),
+        )
+
+        mod_sb = [loads.tile([P, UNIT_TILES, K], BF16, name="mod_sb%d" % u) for u in range(UNITS)]
+        x_sb = [loads.tile([P, UNIT_TILES, K], BF16, name="x_sb%d" % u) for u in range(UNITS)]
+
+        def load_unit(tiles, rows, u):
+            nc.sync.dma_start(out=tiles[u][:], in_=rows[:, u * UNIT_TILES : (u + 1) * UNIT_TILES, :])
+
+        load_unit(mod_sb, mod_rows, 0)
+        modb_rows = const.tile([P, P], BF16)
+        nc.vector.memset(modb_rows[:], 0.0)
+        nc.sync.dma_start(out=modb_rows[0:PACK, :], in_=mod_b.rearrange("(t p) -> t p", p=P))
+        load_unit(x_sb, x_rows, 0)
+        load_unit(mod_sb, mod_rows, 1)
+        w_sb = loads.tile([P, PACK, K], BF16)
+        nc.sync.dma_start(out=w_sb[:], in_=weight.rearrange("(c p) k -> p c k", p=P))
+        bias_rows = const.tile([P, FEATURES], BF16)
+        nc.vector.memset(bias_rows[:], 0.0)
+        nc.sync.dma_start(out=bias_rows[0:1, :], in_=bias.rearrange("(o n) -> o n", o=1))
+        load_unit(x_sb, x_rows, 1)
+        for u in range(2, UNITS):
+            load_unit(mod_sb, mod_rows, u)
+            load_unit(x_sb, x_rows, u)
+
+        ident_f32 = const.tile([P, P], F32)
+        make_identity(nc, ident_f32[:])
+        ident_bf16 = const.tile([P, P], BF16)
+        make_identity(nc, ident_bf16[:])
+        ones = const.tile([P, P], BF16)
+        nc.vector.memset(ones[:], 1.0)
+        eps = const.tile([P, 1], F32)
+        nc.vector.memset(eps[:], EPS)
+        table_warmer = const.tile([P, 1], F32)
+        nc.scalar.activation(out=table_warmer[:], in_=eps[:], func=ACT.Abs_reciprocal_sqrt)
+
+        modb_t = psum.tile([P, P], BF16, tag="tr")
+        nc.tensor.transpose(modb_t[:], modb_rows[:], ident_bf16[:])
+        modb_col = const.tile([P, PACK], F32)
+        nc.vector.tensor_copy(out=modb_col[:], in_=modb_t[:, 0:PACK])
+
+        bias_all = const.tile([P, FEATURES], F32)
+
+        def prepare_bias():
+            bias_ps = psum.tile([P, FEATURES], F32, tag="s")
+            nc.tensor.matmul(out=bias_ps[:], lhsT=ones[:], rhs=bias_rows[:], start=True, stop=True)
+            nc.vector.tensor_copy(out=bias_all[:], in_=bias_ps[:])
+
+        w_grouped = const.tile([P, FEATURES, PACK], BF16, align_bytes=64)
+        w2_grouped = const.tile([P, FEATURES, PACK], BF16, align_bytes=64)
+        w_codes = const.tile([P, FEATURES], U32, align_bytes=64)
+        w_scales = const.tile([P, FEATURES], U8, align_bytes=64)
+        w2_codes = const.tile([P, FEATURES], U32, align_bytes=64)
+        w2_scales = const.tile([P, FEATURES], U8, align_bytes=64)
+
+        def prepare_weight():
+            for half, tag in enumerate(("y", "q")):
+                w_t = psum.tile([P, 2, PACK, P], BF16, tag=tag, name="w_t")
+                for c in range(2):
+                    for t in range(PACK):
+                        nc.tensor.transpose(
+                            w_t[:, c, t, :], w_sb[:, 2 * half + c, t * P : (t + 1) * P], ident_bf16[:]
+                        )
+                nc.scalar.copy(
+                    out=w_grouped[:, 2 * half * P : 2 * (half + 1) * P, :].rearrange(
+                        "p (c r) t -> p c r t", c=2
+                    ),
+                    in_=w_t[:].rearrange("p c t r -> p c r t"),
+                )
+            nc.vector.tensor_tensor(out=w2_grouped[:], in0=w_grouped[:], in1=w_grouped[:], op=ALU.mult)
+            nc.vector.quantize_mx(
+                out=w_codes[:].bitcast(FP8X4),
+                scales=w_scales[:],
+                in_=w_grouped[:].rearrange("p o t -> p (o t)"),
+            )
+            nc.vector.quantize_mx(
+                out=w2_codes[:].bitcast(FP8X4),
+                scales=w2_scales[:],
+                in_=w2_grouped[:].rearrange("p o t -> p (o t)"),
+            )
+
+        def quantise_unit(grouped, what):
+            codes = work.tile([P, UNIT], U32, align_bytes=64, name=what + "_codes")
+            scales = work.tile([P, UNIT], U8, align_bytes=64, name=what + "_scales")
+            nc.vector.quantize_mx(
+                out=codes[:].bitcast(FP8X4),
+                scales=scales[:],
+                in_=grouped[:].rearrange("p r t -> p (r t)"),
+            )
+            return codes, scales
+
+        mod_q = {}
+        s_of = {}
+        x_t_of = {}
+        xs_q = {}
+        ss_q = {}
+
+        def quantise_modulation(u):
+            words = mod_sb[u][:].bitcast(F32)
+            mod_t = psum.tile([P, UNIT_TILES, 2, P], F32, tag="tr")
+            for j in range(UNIT_TILES):
+                for h in range(2):
+                    nc.tensor.transpose(mod_t[:, j, h, :], words[:, j, h : K // 2 : 2], ident_f32[:])
+            mod_grouped = work.tile([P, UNIT, PACK], BF16, align_bytes=64)
+            nc.scalar.copy(
+                out=mod_grouped[:].bitcast(F32).rearrange("p (j r) h -> p j r h", j=UNIT_TILES),
+                in_=mod_t[:].rearrange("p j h r -> p j r h"),
+            )
+            mod_q[u] = quantise_unit(mod_grouped, "mod")
+
+        def compute_s(u):
+            codes, scales = mod_q[u]
+            s_sb = work.tile([P, PACK, UNIT], F32)
+            for t in range(PACK):
+                s_ps = psum.tile([P, UNIT], F32, tag="s")
+                nc.tensor.matmul_mx(
+                    out=s_ps[:],
+                    lhsT=w1_codes[:, t * P : (t + 1) * P].bitcast(FP8X4),
+                    lhsT_scale=w1_scales[:, t * P : (t + 1) * P],
+                    rhs=codes[:].bitcast(FP8X4),
+                    rhs_scale=scales[:],
+                    start=True,
+                    stop=True,
+                )
+                nc.scalar.activation(
+                    out=s_sb[:, t, :], in_=s_ps[:], func=ACT.Identity, bias=modb_col[:, t : t + 1], scale=1.0
+                )
+            s_of[u] = s_sb
+
+        def transpose_x(u):
+            x_t = psum.tile([P, UNIT_TILES, PACK, P], BF16, tag="tr")
+            for j in range(UNIT_TILES):
+                for t in range(PACK):
+                    nc.tensor.transpose(x_t[:, j, t, :], x_sb[u][:, j, t * P : (t + 1) * P], ident_bf16[:])
+            x_t_of[u] = x_t
+
+        def quantise_products(u):
+            s_sb = s_of[u]
+            xs_grouped = work.tile([P, UNIT, PACK], BF16, align_bytes=64)
+            nc.vector.tensor_tensor(
+                out=xs_grouped[:].rearrange("p (j r) t -> p j r t", j=UNIT_TILES),
+                in0=x_t_of[u][:].rearrange("p j t r -> p j r t"),
+                in1=s_sb[:].rearrange("p t (j r) -> p j r t", j=UNIT_TILES),
+                op=ALU.mult,
+            )
+            ss_grouped = work.tile([P, UNIT, PACK], BF16, align_bytes=64)
+            nc.scalar.activation(out=ss_grouped[:], in_=s_sb[:].rearrange("p t r -> p r t"), func=ACT.Square)
+            xs_q[u] = quantise_unit(xs_grouped, "xs")
+            ss_q[u] = quantise_unit(ss_grouped, "ss")
+
+        def finish(u):
+            xs_codes, xs_scales = xs_q[u]
+            ss_codes, ss_scales = ss_q[u]
+            result = work.tile([P, UNIT_TILES, FEATURES], F32)
+            for j in range(UNIT_TILES):
+                cols = slice(j * P, (j + 1) * P)
+                q_ps = psum.tile([P, FEATURES], F32, tag="q")
+                nc.tensor.matmul_mx(
+                    out=q_ps[:],
+                    lhsT=ss_codes[:, cols].bitcast(FP8X4),
+                    lhsT_scale=ss_scales[:, cols],
+                    rhs=w2_codes[:].bitcast(FP8X4),
+                    rhs_scale=w2_scales[:],
+                    start=True,
+                    stop=True,
+                )
+                y_ps = psum.tile([P, FEATURES], F32, tag="y")
+                nc.tensor.matmul_mx(
+                    out=y_ps[:],
+                    lhsT=xs_codes[:, cols].bitcast(FP8X4),
+                    lhsT_scale=xs_scales[:, cols],
+                    rhs=w_codes[:].bitcast(FP8X4),
+                    rhs_scale=w_scales[:],
+                    start=True,
+                    stop=True,
+                )
+                demod = work.tile([P, FEATURES], F32)
+                nc.scalar.activation(
+                    out=demod[:], in_=q_ps[:], func=ACT.Abs_reciprocal_sqrt, bias=eps[:], scale=1.0
+                )
+                nc.vector.tensor_tensor(out=result[:, j, :], in0=y_ps[:], in1=demod[:], op=ALU.mult)
+            nc.vector.tensor_tensor(
+                out=result[:],
+                in0=result[:],
+                in1=bias_all[:].unsqueeze(1).to_broadcast([P, UNIT_TILES, FEATURES]),
+                op=ALU.add,
+            )
+            nc.sync.dma_start(out=out_rows[:, u * UNIT_TILES : (u + 1) * UNIT_TILES, :], in_=result[:])
+
+        for i in range(UNITS + 3):
+            if 0 <= i - 2 < UNITS:
+                quantise_products(i - 2)
+            if 0 <= i - 3 < UNITS:
+                finish(i - 3)
+            if i < UNITS:
+                quantise_modulation(i)
+            if 0 <= i - 1 < UNITS:
+                transpose_x(i - 1)
+                compute_s(i - 1)
+            if i == WEIGHT_ROUND:
+                prepare_weight()
+                prepare_bias()

@@ -21,8 +21,8 @@ TILES = TOKENS // P
 UNIT_TILES = 2
 UNIT = UNIT_TILES * P
 UNITS = TILES // UNIT_TILES
+STAGES = 5
 EPS = 1e-8
-WEIGHT_ROUND = 1
 
 FLOPS = 3 * 2 * TOKENS * K * FEATURES
 
@@ -36,11 +36,19 @@ def tile_modulatedlinear_kernel(
     out_rows = out.flatten_outer_dims().rearrange("(p j) n -> p j n", j=TILES)
 
     with ExitStack() as ctx:
+        ctx.enter_context(tc.manual_schedule())
         const = ctx.enter_context(tc.tile_pool(name="const", bufs=1))
         loads = ctx.enter_context(tc.tile_pool(name="loads", bufs=1))
         work = ctx.enter_context(tc.tile_pool(name="work", bufs=3))
         psum = ctx.enter_context(tc.psum_pool(name="psum", bufs=2))
 
+        mod_sb = [loads.tile([P, UNIT_TILES, K], BF16, name="mod_sb%d" % u) for u in range(UNITS)]
+        x_sb = [loads.tile([P, UNIT_TILES, K], BF16, name="x_sb%d" % u) for u in range(UNITS)]
+
+        def load_unit(tiles, rows, u):
+            nc.sync.dma_start(out=tiles[u][:], in_=rows[:, u * UNIT_TILES : (u + 1) * UNIT_TILES, :])
+
+        load_unit(mod_sb, mod_rows, 0)
         w1_scales = const.tile([P, FEATURES], U8, align_bytes=64)
         nc.vector.memset(w1_scales[:].bitcast(I32), 0)
         for quadrant in range(4):
@@ -53,31 +61,23 @@ def tile_modulatedlinear_kernel(
             out=w1_codes[:].bitcast(I32),
             in_=mod_w_words[0].rearrange("p n t -> p (n t)").bitcast(I32),
         )
-
-        mod_sb = [loads.tile([P, UNIT_TILES, K], BF16, name="mod_sb%d" % u) for u in range(UNITS)]
-        x_sb = [loads.tile([P, UNIT_TILES, K], BF16, name="x_sb%d" % u) for u in range(UNITS)]
-
-        def load_unit(tiles, rows, u):
-            nc.sync.dma_start(out=tiles[u][:], in_=rows[:, u * UNIT_TILES : (u + 1) * UNIT_TILES, :])
-
-        load_unit(mod_sb, mod_rows, 0)
-        modb_rows = const.tile([P, P], BF16)
-        nc.vector.memset(modb_rows[:], 0.0)
-        nc.sync.dma_start(out=modb_rows[0:PACK, :], in_=mod_b.rearrange("(t p) -> t p", p=P))
-        load_unit(x_sb, x_rows, 0)
-        load_unit(mod_sb, mod_rows, 1)
         w_sb = loads.tile([P, PACK, K], BF16)
         nc.sync.dma_start(out=w_sb[:], in_=weight.rearrange("(c p) k -> p c k", p=P))
-        bias_rows = const.tile([P, FEATURES], BF16)
-        nc.vector.memset(bias_rows[:], 0.0)
-        nc.sync.dma_start(out=bias_rows[0:1, :], in_=bias.rearrange("(o n) -> o n", o=1))
-        load_unit(x_sb, x_rows, 1)
+        load_unit(mod_sb, mod_rows, 1)
+        load_unit(x_sb, x_rows, 0)
         for u in range(2, UNITS):
             load_unit(mod_sb, mod_rows, u)
-            load_unit(x_sb, x_rows, u)
+            load_unit(x_sb, x_rows, u - 1)
+        load_unit(x_sb, x_rows, UNITS - 1)
 
         ident_f32 = const.tile([P, P], F32)
         make_identity(nc, ident_f32[:])
+        modb_rows = const.tile([P, P], BF16)
+        nc.vector.memset(modb_rows[:], 0.0)
+        nc.gpsimd.dma_start(out=modb_rows[0:PACK, :], in_=mod_b.rearrange("(t p) -> t p", p=P))
+        bias_rows = const.tile([P, FEATURES], BF16)
+        nc.vector.memset(bias_rows[:], 0.0)
+        nc.gpsimd.dma_start(out=bias_rows[0:1, :], in_=bias.rearrange("(o n) -> o n", o=1))
         ident_bf16 = const.tile([P, P], BF16)
         make_identity(nc, ident_bf16[:])
         ones = const.tile([P, P], BF16)
@@ -87,15 +87,14 @@ def tile_modulatedlinear_kernel(
         table_warmer = const.tile([P, 1], F32)
         nc.scalar.activation(out=table_warmer[:], in_=eps[:], func=ACT.Abs_reciprocal_sqrt)
 
-        modb_t = psum.tile([P, P], BF16, tag="tr")
-        nc.tensor.transpose(modb_t[:], modb_rows[:], ident_bf16[:])
         modb_col = const.tile([P, PACK], F32)
-        nc.vector.tensor_copy(out=modb_col[:], in_=modb_t[:, 0:PACK])
-
         bias_all = const.tile([P, FEATURES], F32)
 
-        def prepare_bias():
-            bias_ps = psum.tile([P, FEATURES], F32, tag="s")
+        def spread_vectors():
+            modb_t = psum.tile([P, P], BF16, tag="x_t", bufs=1)
+            nc.tensor.transpose(modb_t[:], modb_rows[:], ident_bf16[:])
+            nc.vector.tensor_copy(out=modb_col[:], in_=modb_t[:, 0:PACK])
+            bias_ps = psum.tile([P, FEATURES], F32, tag="x_t", bufs=1)
             nc.tensor.matmul(out=bias_ps[:], lhsT=ones[:], rhs=bias_rows[:], start=True, stop=True)
             nc.vector.tensor_copy(out=bias_all[:], in_=bias_ps[:])
 
@@ -105,21 +104,25 @@ def tile_modulatedlinear_kernel(
         w_scales = const.tile([P, FEATURES], U8, align_bytes=64)
         w2_codes = const.tile([P, FEATURES], U32, align_bytes=64)
         w2_scales = const.tile([P, FEATURES], U8, align_bytes=64)
+        w_t_of = {}
 
-        def prepare_weight():
-            for half, tag in enumerate(("y", "q")):
+        def transpose_weight():
+            for half, tag in enumerate(("q", "y")):
                 w_t = psum.tile([P, 2, PACK, P], BF16, tag=tag, name="w_t")
                 for c in range(2):
                     for t in range(PACK):
                         nc.tensor.transpose(
                             w_t[:, c, t, :], w_sb[:, 2 * half + c, t * P : (t + 1) * P], ident_bf16[:]
                         )
-                nc.scalar.copy(
-                    out=w_grouped[:, 2 * half * P : 2 * (half + 1) * P, :].rearrange(
-                        "p (c r) t -> p c r t", c=2
-                    ),
-                    in_=w_t[:].rearrange("p c t r -> p c r t"),
-                )
+                w_t_of[half] = w_t
+
+        def group_weight(half, copy):
+            copy(
+                out=w_grouped[:, 2 * half * P : 2 * (half + 1) * P, :].rearrange("p (c r) t -> p c r t", c=2),
+                in_=w_t_of[half][:].rearrange("p c t r -> p c r t"),
+            )
+
+        def quantise_weight():
             nc.vector.tensor_tensor(out=w2_grouped[:], in0=w_grouped[:], in1=w_grouped[:], op=ALU.mult)
             nc.vector.quantize_mx(
                 out=w_codes[:].bitcast(FP8X4),
@@ -142,24 +145,33 @@ def tile_modulatedlinear_kernel(
             )
             return codes, scales
 
+        mod_t_of = {}
+        mod_grouped_of = {}
         mod_q = {}
         s_of = {}
         x_t_of = {}
+        xs_grouped_of = {}
+        ss_grouped_of = {}
         xs_q = {}
         ss_q = {}
+        y_of = {}
+        demod_of = {}
 
-        def quantise_modulation(u):
+        def transpose_modulation(u):
             words = mod_sb[u][:].bitcast(F32)
-            mod_t = psum.tile([P, UNIT_TILES, 2, P], F32, tag="tr")
+            mod_t = psum.tile([P, UNIT_TILES, 2, P], F32, tag="mod_t", bufs=1)
             for j in range(UNIT_TILES):
                 for h in range(2):
                     nc.tensor.transpose(mod_t[:, j, h, :], words[:, j, h : K // 2 : 2], ident_f32[:])
+            mod_t_of[u] = mod_t
+
+        def group_modulation(u):
             mod_grouped = work.tile([P, UNIT, PACK], BF16, align_bytes=64)
             nc.scalar.copy(
                 out=mod_grouped[:].bitcast(F32).rearrange("p (j r) h -> p j r h", j=UNIT_TILES),
-                in_=mod_t[:].rearrange("p j h r -> p j r h"),
+                in_=mod_t_of[u][:].rearrange("p j h r -> p j r h"),
             )
-            mod_q[u] = quantise_unit(mod_grouped, "mod")
+            mod_grouped_of[u] = mod_grouped
 
         def compute_s(u):
             codes, scales = mod_q[u]
@@ -181,30 +193,33 @@ def tile_modulatedlinear_kernel(
             s_of[u] = s_sb
 
         def transpose_x(u):
-            x_t = psum.tile([P, UNIT_TILES, PACK, P], BF16, tag="tr")
+            x_t = psum.tile([P, PACK, UNIT], BF16, tag="x_t", bufs=1)
             for j in range(UNIT_TILES):
                 for t in range(PACK):
-                    nc.tensor.transpose(x_t[:, j, t, :], x_sb[u][:, j, t * P : (t + 1) * P], ident_bf16[:])
+                    nc.tensor.transpose(
+                        x_t[:, t, j * P : (j + 1) * P], x_sb[u][:, j, t * P : (t + 1) * P], ident_bf16[:]
+                    )
             x_t_of[u] = x_t
 
-        def quantise_products(u):
+        def multiply(u):
             s_sb = s_of[u]
             xs_grouped = work.tile([P, UNIT, PACK], BF16, align_bytes=64)
             nc.vector.tensor_tensor(
-                out=xs_grouped[:].rearrange("p (j r) t -> p j r t", j=UNIT_TILES),
-                in0=x_t_of[u][:].rearrange("p j t r -> p j r t"),
-                in1=s_sb[:].rearrange("p t (j r) -> p j r t", j=UNIT_TILES),
+                out=xs_grouped[:],
+                in0=x_t_of[u][:].rearrange("p t r -> p r t"),
+                in1=s_sb[:].rearrange("p t r -> p r t"),
                 op=ALU.mult,
             )
             ss_grouped = work.tile([P, UNIT, PACK], BF16, align_bytes=64)
-            nc.scalar.activation(out=ss_grouped[:], in_=s_sb[:].rearrange("p t r -> p r t"), func=ACT.Square)
-            xs_q[u] = quantise_unit(xs_grouped, "xs")
-            ss_q[u] = quantise_unit(ss_grouped, "ss")
+            nc.scalar.activation(
+                out=ss_grouped[:], in_=s_sb[:].rearrange("p t r -> p r t"), func=ACT.Square
+            )
+            xs_grouped_of[u] = xs_grouped
+            ss_grouped_of[u] = ss_grouped
 
-        def finish(u):
+        def demodulation(u):
             xs_codes, xs_scales = xs_q[u]
             ss_codes, ss_scales = ss_q[u]
-            result = work.tile([P, UNIT_TILES, FEATURES], F32)
             for j in range(UNIT_TILES):
                 cols = slice(j * P, (j + 1) * P)
                 q_ps = psum.tile([P, FEATURES], F32, tag="q")
@@ -231,25 +246,43 @@ def tile_modulatedlinear_kernel(
                 nc.scalar.activation(
                     out=demod[:], in_=q_ps[:], func=ACT.Abs_reciprocal_sqrt, bias=eps[:], scale=1.0
                 )
-                nc.vector.tensor_tensor(out=result[:, j, :], in0=y_ps[:], in1=demod[:], op=ALU.mult)
-            nc.vector.tensor_tensor(
-                out=result[:],
-                in0=result[:],
-                in1=bias_all[:].unsqueeze(1).to_broadcast([P, UNIT_TILES, FEATURES]),
-                op=ALU.add,
-            )
-            nc.sync.dma_start(out=out_rows[:, u * UNIT_TILES : (u + 1) * UNIT_TILES, :], in_=result[:])
+                y_of[u, j] = y_ps
+                demod_of[u, j] = demod
 
-        for i in range(UNITS + 3):
-            if 0 <= i - 2 < UNITS:
-                quantise_products(i - 2)
-            if 0 <= i - 3 < UNITS:
-                finish(i - 3)
-            if i < UNITS:
-                quantise_modulation(i)
-            if 0 <= i - 1 < UNITS:
-                transpose_x(i - 1)
+        def finish(u):
+            for j in range(UNIT_TILES):
+                result = work.tile([P, FEATURES], F32, bufs=2 * UNIT_TILES)
+                nc.vector.tensor_tensor(out=result[:], in0=y_of[u, j][:], in1=demod_of[u, j][:], op=ALU.mult)
+                nc.vector.tensor_tensor(out=result[:], in0=result[:], in1=bias_all[:], op=ALU.add)
+                nc.sync.dma_start(out=out_rows[:, u * UNIT_TILES + j, :], in_=result[:])
+
+        def live(u):
+            return 0 <= u < UNITS
+
+        for i in range(UNITS + STAGES - 1):
+            if live(i):
+                transpose_modulation(i)
+            if live(i - 2):
+                transpose_x(i - 2)
+            if live(i - 1):
+                mod_q[i - 1] = quantise_unit(mod_grouped_of[i - 1], "mod")
+            if live(i - 3):
+                xs_q[i - 3] = quantise_unit(xs_grouped_of[i - 3], "xs")
+                ss_q[i - 3] = quantise_unit(ss_grouped_of[i - 3], "ss")
+            if i == 1:
+                group_weight(1, nc.vector.tensor_copy)
+                quantise_weight()
+            if live(i - 4):
+                finish(i - 4)
+            if live(i - 2):
+                multiply(i - 2)
+            if live(i):
+                group_modulation(i)
+            if i == 0:
+                spread_vectors()
+                transpose_weight()
+                group_weight(0, nc.scalar.copy)
+            if live(i - 1):
                 compute_s(i - 1)
-            if i == WEIGHT_ROUND:
-                prepare_weight()
-                prepare_bias()
+            if live(i - 3):
+                demodulation(i - 3)

@@ -22,6 +22,7 @@ UNIT_TILES = 2
 UNIT = UNIT_TILES * P
 UNITS = TILES // UNIT_TILES
 STAGES = 5
+RUN = 4
 EPS = 1e-8
 
 FLOPS = 3 * 2 * TOKENS * K * FEATURES
@@ -36,7 +37,6 @@ def tile_modulatedlinear_kernel(
     out_rows = out.flatten_outer_dims().rearrange("(p j) n -> p j n", j=TILES)
 
     with ExitStack() as ctx:
-        ctx.enter_context(tc.manual_schedule())
         const = ctx.enter_context(tc.tile_pool(name="const", bufs=1))
         loads = ctx.enter_context(tc.tile_pool(name="loads", bufs=1))
         work = ctx.enter_context(tc.tile_pool(name="work", bufs=3))
@@ -49,6 +49,8 @@ def tile_modulatedlinear_kernel(
             nc.sync.dma_start(out=tiles[u][:], in_=rows[:, u * UNIT_TILES : (u + 1) * UNIT_TILES, :])
 
         load_unit(mod_sb, mod_rows, 0)
+        w_sb = loads.tile([P, PACK, K], BF16)
+        nc.sync.dma_start(out=w_sb[:], in_=weight.rearrange("(c p) k -> p c k", p=P))
         w1_scales = const.tile([P, FEATURES], U8, align_bytes=64)
         nc.vector.memset(w1_scales[:].bitcast(I32), 0)
         for quadrant in range(4):
@@ -61,23 +63,23 @@ def tile_modulatedlinear_kernel(
             out=w1_codes[:].bitcast(I32),
             in_=mod_w_words[0].rearrange("p n t -> p (n t)").bitcast(I32),
         )
-        w_sb = loads.tile([P, PACK, K], BF16)
-        nc.sync.dma_start(out=w_sb[:], in_=weight.rearrange("(c p) k -> p c k", p=P))
+        modb_rows = const.tile([P, P], BF16)
+        nc.vector.memset(modb_rows[:], 0.0)
+        nc.sync.dma_start(out=modb_rows[0:PACK, :], in_=mod_b.rearrange("(t p) -> t p", p=P))
         load_unit(mod_sb, mod_rows, 1)
         load_unit(x_sb, x_rows, 0)
-        for u in range(2, UNITS):
+        load_unit(mod_sb, mod_rows, 2)
+        load_unit(x_sb, x_rows, 1)
+        bias_rows = const.tile([P, FEATURES], BF16)
+        nc.vector.memset(bias_rows[:], 0.0)
+        nc.sync.dma_start(out=bias_rows[0:1, :], in_=bias.rearrange("(o n) -> o n", o=1))
+        for u in range(3, UNITS):
             load_unit(mod_sb, mod_rows, u)
             load_unit(x_sb, x_rows, u - 1)
         load_unit(x_sb, x_rows, UNITS - 1)
 
         ident_f32 = const.tile([P, P], F32)
         make_identity(nc, ident_f32[:])
-        modb_rows = const.tile([P, P], BF16)
-        nc.vector.memset(modb_rows[:], 0.0)
-        nc.gpsimd.dma_start(out=modb_rows[0:PACK, :], in_=mod_b.rearrange("(t p) -> t p", p=P))
-        bias_rows = const.tile([P, FEATURES], BF16)
-        nc.vector.memset(bias_rows[:], 0.0)
-        nc.gpsimd.dma_start(out=bias_rows[0:1, :], in_=bias.rearrange("(o n) -> o n", o=1))
         ident_bf16 = const.tile([P, P], BF16)
         make_identity(nc, ident_bf16[:])
         ones = const.tile([P, P], BF16)
@@ -90,13 +92,15 @@ def tile_modulatedlinear_kernel(
         modb_col = const.tile([P, PACK], F32)
         bias_all = const.tile([P, FEATURES], F32)
 
-        def spread_vectors():
+        def spread_mod_b():
             modb_t = psum.tile([P, P], BF16, tag="x_t", bufs=1)
             nc.tensor.transpose(modb_t[:], modb_rows[:], ident_bf16[:])
             nc.vector.tensor_copy(out=modb_col[:], in_=modb_t[:, 0:PACK])
+
+        def spread_bias():
             bias_ps = psum.tile([P, FEATURES], F32, tag="x_t", bufs=1)
             nc.tensor.matmul(out=bias_ps[:], lhsT=ones[:], rhs=bias_rows[:], start=True, stop=True)
-            nc.vector.tensor_copy(out=bias_all[:], in_=bias_ps[:])
+            nc.scalar.copy(out=bias_all[:], in_=bias_ps[:])
 
         w_grouped = const.tile([P, FEATURES, PACK], BF16, align_bytes=64)
         w2_grouped = const.tile([P, FEATURES, PACK], BF16, align_bytes=64)
@@ -104,9 +108,8 @@ def tile_modulatedlinear_kernel(
         w_scales = const.tile([P, FEATURES], U8, align_bytes=64)
         w2_codes = const.tile([P, FEATURES], U32, align_bytes=64)
         w2_scales = const.tile([P, FEATURES], U8, align_bytes=64)
-        w_t_of = {}
 
-        def transpose_weight():
+        def group_weight():
             for half, tag in enumerate(("q", "y")):
                 w_t = psum.tile([P, 2, PACK, P], BF16, tag=tag, name="w_t")
                 for c in range(2):
@@ -114,13 +117,10 @@ def tile_modulatedlinear_kernel(
                         nc.tensor.transpose(
                             w_t[:, c, t, :], w_sb[:, 2 * half + c, t * P : (t + 1) * P], ident_bf16[:]
                         )
-                w_t_of[half] = w_t
-
-        def group_weight(half, copy):
-            copy(
-                out=w_grouped[:, 2 * half * P : 2 * (half + 1) * P, :].rearrange("p (c r) t -> p c r t", c=2),
-                in_=w_t_of[half][:].rearrange("p c t r -> p c r t"),
-            )
+                nc.scalar.copy(
+                    out=w_grouped[:, 2 * half * P : 2 * (half + 1) * P, :].rearrange("p (c r) t -> p c r t", c=2),
+                    in_=w_t[:].rearrange("p c t r -> p c r t"),
+                )
 
         def quantise_weight():
             nc.vector.tensor_tensor(out=w2_grouped[:], in0=w_grouped[:], in1=w_grouped[:], op=ALU.mult)
@@ -167,7 +167,7 @@ def tile_modulatedlinear_kernel(
 
         def group_modulation(u):
             mod_grouped = work.tile([P, UNIT, PACK], BF16, align_bytes=64)
-            nc.scalar.copy(
+            nc.vector.tensor_copy(
                 out=mod_grouped[:].bitcast(F32).rearrange("p (j r) h -> p j r h", j=UNIT_TILES),
                 in_=mod_t_of[u][:].rearrange("p j h r -> p j r h"),
             )
@@ -176,20 +176,26 @@ def tile_modulatedlinear_kernel(
         def compute_s(u):
             codes, scales = mod_q[u]
             s_sb = work.tile([P, PACK, UNIT], F32)
-            for t in range(PACK):
-                s_ps = psum.tile([P, UNIT], F32, tag="s")
-                nc.tensor.matmul_mx(
-                    out=s_ps[:],
-                    lhsT=w1_codes[:, t * P : (t + 1) * P].bitcast(FP8X4),
-                    lhsT_scale=w1_scales[:, t * P : (t + 1) * P],
-                    rhs=codes[:].bitcast(FP8X4),
-                    rhs_scale=scales[:],
-                    start=True,
-                    stop=True,
-                )
-                nc.scalar.activation(
-                    out=s_sb[:, t, :], in_=s_ps[:], func=ACT.Identity, bias=modb_col[:, t : t + 1], scale=1.0
-                )
+            for pair in range(PACK // 2):
+                s_ps = psum.tile([P, 2, UNIT], F32, tag="s")
+                for t in (2 * pair, 2 * pair + 1):
+                    nc.tensor.matmul_mx(
+                        out=s_ps[:, t % 2, :],
+                        lhsT=w1_codes[:, t * P : (t + 1) * P].bitcast(FP8X4),
+                        lhsT_scale=w1_scales[:, t * P : (t + 1) * P],
+                        rhs=codes[:].bitcast(FP8X4),
+                        rhs_scale=scales[:],
+                        start=True,
+                        stop=True,
+                    )
+                for t in (2 * pair + 1, 2 * pair):
+                    nc.scalar.activation(
+                        out=s_sb[:, t, :],
+                        in_=s_ps[:, t % 2, :],
+                        func=ACT.Identity,
+                        bias=modb_col[:, t : t + 1],
+                        scale=1.0,
+                    )
             s_of[u] = s_sb
 
         def transpose_x(u):
@@ -205,14 +211,14 @@ def tile_modulatedlinear_kernel(
             s_sb = s_of[u]
             xs_grouped = work.tile([P, UNIT, PACK], BF16, align_bytes=64)
             nc.vector.tensor_tensor(
-                out=xs_grouped[:],
-                in0=x_t_of[u][:].rearrange("p t r -> p r t"),
-                in1=s_sb[:].rearrange("p t r -> p r t"),
+                out=xs_grouped[:].rearrange("p (c i) t -> p c t i", i=RUN),
+                in0=x_t_of[u][:].rearrange("p t (c i) -> p c t i", i=RUN),
+                in1=s_sb[:].rearrange("p t (c i) -> p c t i", i=RUN),
                 op=ALU.mult,
             )
             ss_grouped = work.tile([P, UNIT, PACK], BF16, align_bytes=64)
             nc.scalar.activation(
-                out=ss_grouped[:], in_=s_sb[:].rearrange("p t r -> p r t"), func=ACT.Square
+                out=ss_grouped[:].rearrange("p (c i) t -> p c t i", i=RUN), in_=s_sb[:].rearrange("p t (c i) -> p c t i", i=RUN), func=ACT.Square
             )
             xs_grouped_of[u] = xs_grouped
             ss_grouped_of[u] = ss_grouped
@@ -242,7 +248,7 @@ def tile_modulatedlinear_kernel(
                     start=True,
                     stop=True,
                 )
-                demod = work.tile([P, FEATURES], F32)
+                demod = work.tile([P, FEATURES], F32, bufs=2 * UNIT_TILES)
                 nc.scalar.activation(
                     out=demod[:], in_=q_ps[:], func=ACT.Abs_reciprocal_sqrt, bias=eps[:], scale=1.0
                 )
@@ -253,7 +259,7 @@ def tile_modulatedlinear_kernel(
             for j in range(UNIT_TILES):
                 result = work.tile([P, FEATURES], F32, bufs=2 * UNIT_TILES)
                 nc.vector.tensor_tensor(out=result[:], in0=y_of[u, j][:], in1=demod_of[u, j][:], op=ALU.mult)
-                nc.vector.tensor_tensor(out=result[:], in0=result[:], in1=bias_all[:], op=ALU.add)
+                nc.gpsimd.tensor_tensor(out=result[:], in0=result[:], in1=bias_all[:], op=ALU.add)
                 nc.sync.dma_start(out=out_rows[:, u * UNIT_TILES + j, :], in_=result[:])
 
         def live(u):
@@ -269,8 +275,7 @@ def tile_modulatedlinear_kernel(
             if live(i - 3):
                 xs_q[i - 3] = quantise_unit(xs_grouped_of[i - 3], "xs")
                 ss_q[i - 3] = quantise_unit(ss_grouped_of[i - 3], "ss")
-            if i == 1:
-                group_weight(1, nc.vector.tensor_copy)
+            if i == 2:
                 quantise_weight()
             if live(i - 4):
                 finish(i - 4)
@@ -279,10 +284,11 @@ def tile_modulatedlinear_kernel(
             if live(i):
                 group_modulation(i)
             if i == 0:
-                spread_vectors()
-                transpose_weight()
-                group_weight(0, nc.scalar.copy)
+                spread_mod_b()
+                group_weight()
             if live(i - 1):
                 compute_s(i - 1)
+            if i == 1:
+                spread_bias()
             if live(i - 3):
                 demodulation(i - 3)

@@ -22,6 +22,9 @@ UNIT_TILES = 2
 UNIT = UNIT_TILES * P
 UNITS = TILES // UNIT_TILES
 STAGES = 5
+BIAS_PIECES = 2
+XS = 0
+SS = 1
 RUN = 4
 EPS = 1e-8
 
@@ -135,14 +138,10 @@ def tile_modulatedlinear_kernel(
                 in_=w2_grouped[:].rearrange("p o t -> p (o t)"),
             )
 
-        def quantise_unit(grouped, what):
-            codes = work.tile([P, UNIT], U32, align_bytes=64, name=what + "_codes")
-            scales = work.tile([P, UNIT], U8, align_bytes=64, name=what + "_scales")
-            nc.vector.quantize_mx(
-                out=codes[:].bitcast(FP8X4),
-                scales=scales[:],
-                in_=grouped[:].rearrange("p r t -> p (r t)"),
-            )
+        def quantise(grouped, words, what):
+            codes = work.tile([P, words], U32, align_bytes=64, name=what + "_codes")
+            scales = work.tile([P, words], U8, align_bytes=64, name=what + "_scales")
+            nc.vector.quantize_mx(out=codes[:].bitcast(FP8X4), scales=scales[:], in_=grouped)
             return codes, scales
 
         mod_t_of = {}
@@ -150,10 +149,8 @@ def tile_modulatedlinear_kernel(
         mod_q = {}
         s_of = {}
         x_t_of = {}
-        xs_grouped_of = {}
-        ss_grouped_of = {}
-        xs_q = {}
-        ss_q = {}
+        products_of = {}
+        products_q = {}
         y_of = {}
         demod_of = {}
 
@@ -209,30 +206,28 @@ def tile_modulatedlinear_kernel(
 
         def multiply(u):
             s_sb = s_of[u]
-            xs_grouped = work.tile([P, UNIT, PACK], BF16, align_bytes=64)
+            products = work.tile([P, 2, UNIT, PACK], BF16, align_bytes=64)
             nc.vector.tensor_tensor(
-                out=xs_grouped[:].rearrange("p (c i) t -> p c t i", i=RUN),
+                out=products[:, XS].rearrange("p (c i) t -> p c t i", i=RUN),
                 in0=x_t_of[u][:].rearrange("p t (c i) -> p c t i", i=RUN),
                 in1=s_sb[:].rearrange("p t (c i) -> p c t i", i=RUN),
                 op=ALU.mult,
             )
-            ss_grouped = work.tile([P, UNIT, PACK], BF16, align_bytes=64)
             nc.scalar.activation(
-                out=ss_grouped[:].rearrange("p (c i) t -> p c t i", i=RUN), in_=s_sb[:].rearrange("p t (c i) -> p c t i", i=RUN), func=ACT.Square
+                out=products[:, SS].rearrange("p (c i) t -> p c t i", i=RUN), in_=s_sb[:].rearrange("p t (c i) -> p c t i", i=RUN), func=ACT.Square
             )
-            xs_grouped_of[u] = xs_grouped
-            ss_grouped_of[u] = ss_grouped
+            products_of[u] = products
 
         def demodulation(u):
-            xs_codes, xs_scales = xs_q[u]
-            ss_codes, ss_scales = ss_q[u]
+            codes, scales = products_q[u]
             for j in range(UNIT_TILES):
-                cols = slice(j * P, (j + 1) * P)
+                xs_cols = slice(XS * UNIT + j * P, XS * UNIT + (j + 1) * P)
+                ss_cols = slice(SS * UNIT + j * P, SS * UNIT + (j + 1) * P)
                 q_ps = psum.tile([P, FEATURES], F32, tag="q")
                 nc.tensor.matmul_mx(
                     out=q_ps[:],
-                    lhsT=ss_codes[:, cols].bitcast(FP8X4),
-                    lhsT_scale=ss_scales[:, cols],
+                    lhsT=codes[:, ss_cols].bitcast(FP8X4),
+                    lhsT_scale=scales[:, ss_cols],
                     rhs=w2_codes[:].bitcast(FP8X4),
                     rhs_scale=w2_scales[:],
                     start=True,
@@ -241,8 +236,8 @@ def tile_modulatedlinear_kernel(
                 y_ps = psum.tile([P, FEATURES], F32, tag="y")
                 nc.tensor.matmul_mx(
                     out=y_ps[:],
-                    lhsT=xs_codes[:, cols].bitcast(FP8X4),
-                    lhsT_scale=xs_scales[:, cols],
+                    lhsT=codes[:, xs_cols].bitcast(FP8X4),
+                    lhsT_scale=scales[:, xs_cols],
                     rhs=w_codes[:].bitcast(FP8X4),
                     rhs_scale=w_scales[:],
                     start=True,
@@ -259,7 +254,9 @@ def tile_modulatedlinear_kernel(
             for j in range(UNIT_TILES):
                 result = work.tile([P, FEATURES], F32, bufs=2 * UNIT_TILES)
                 nc.vector.tensor_tensor(out=result[:], in0=y_of[u, j][:], in1=demod_of[u, j][:], op=ALU.mult)
-                nc.gpsimd.tensor_tensor(out=result[:], in0=result[:], in1=bias_all[:], op=ALU.add)
+                for piece in range(BIAS_PIECES):
+                    cols = slice(piece * FEATURES // BIAS_PIECES, (piece + 1) * FEATURES // BIAS_PIECES)
+                    nc.gpsimd.tensor_tensor(out=result[:, cols], in0=result[:, cols], in1=bias_all[:, cols], op=ALU.add)
                 nc.sync.dma_start(out=out_rows[:, u * UNIT_TILES + j, :], in_=result[:])
 
         def live(u):
@@ -271,10 +268,11 @@ def tile_modulatedlinear_kernel(
             if live(i - 2):
                 transpose_x(i - 2)
             if live(i - 1):
-                mod_q[i - 1] = quantise_unit(mod_grouped_of[i - 1], "mod")
+                mod_q[i - 1] = quantise(mod_grouped_of[i - 1][:].rearrange("p r t -> p (r t)"), UNIT, "mod")
             if live(i - 3):
-                xs_q[i - 3] = quantise_unit(xs_grouped_of[i - 3], "xs")
-                ss_q[i - 3] = quantise_unit(ss_grouped_of[i - 3], "ss")
+                products_q[i - 3] = quantise(
+                    products_of[i - 3][:].rearrange("p a r t -> p (a r t)"), 2 * UNIT, "products"
+                )
             if i == 2:
                 quantise_weight()
             if live(i - 4):

@@ -22,6 +22,8 @@ UNIT_TILES = 2
 UNIT = UNIT_TILES * P
 UNITS = TILES // UNIT_TILES
 STAGES = 5
+RESULT_BUFS = 8
+VECTOR_BIAS_UNITS = 2
 BIAS_PIECES = 2
 XS = 0
 SS = 1
@@ -164,7 +166,8 @@ def tile_modulatedlinear_kernel(
 
         def group_modulation(u):
             mod_grouped = work.tile([P, UNIT, PACK], BF16, align_bytes=64)
-            nc.vector.tensor_copy(
+            copy = nc.vector.tensor_copy if u % 2 == 0 else nc.scalar.copy
+            copy(
                 out=mod_grouped[:].bitcast(F32).rearrange("p (j r) h -> p j r h", j=UNIT_TILES),
                 in_=mod_t_of[u][:].rearrange("p j h r -> p j r h"),
             )
@@ -245,18 +248,23 @@ def tile_modulatedlinear_kernel(
                 )
                 demod = work.tile([P, FEATURES], F32, bufs=2 * UNIT_TILES)
                 nc.scalar.activation(
-                    out=demod[:], in_=q_ps[:], func=ACT.Abs_reciprocal_sqrt, bias=eps[:], scale=1.0
+                    out=demod[:], in_=q_ps[:], func=ACT.Abs_reciprocal_sqrt, bias=EPS, scale=1.0
                 )
                 y_of[u, j] = y_ps
                 demod_of[u, j] = demod
 
         def finish(u):
             for j in range(UNIT_TILES):
-                result = work.tile([P, FEATURES], F32, bufs=2 * UNIT_TILES)
+                result = work.tile([P, FEATURES], F32, bufs=RESULT_BUFS)
                 nc.vector.tensor_tensor(out=result[:], in0=y_of[u, j][:], in1=demod_of[u, j][:], op=ALU.mult)
-                for piece in range(BIAS_PIECES):
-                    cols = slice(piece * FEATURES // BIAS_PIECES, (piece + 1) * FEATURES // BIAS_PIECES)
-                    nc.gpsimd.tensor_tensor(out=result[:, cols], in0=result[:, cols], in1=bias_all[:, cols], op=ALU.add)
+                if u >= UNITS - VECTOR_BIAS_UNITS:
+                    nc.vector.tensor_tensor(out=result[:], in0=result[:], in1=bias_all[:], op=ALU.add)
+                else:
+                    for piece in range(BIAS_PIECES):
+                        cols = slice(piece * FEATURES // BIAS_PIECES, (piece + 1) * FEATURES // BIAS_PIECES)
+                        nc.gpsimd.tensor_tensor(
+                            out=result[:, cols], in0=result[:, cols], in1=bias_all[:, cols], op=ALU.add
+                        )
                 nc.sync.dma_start(out=out_rows[:, u * UNIT_TILES + j, :], in_=result[:])
 
         def live(u):

@@ -28,6 +28,7 @@ BIAS_PIECES = 2
 XS = 0
 SS = 1
 RUN = 4
+BIAS_LOAD_BEHIND = 4
 EPS = 1e-8
 
 FLOPS = 3 * 2 * TOKENS * K * FEATURES
@@ -75,37 +76,29 @@ def tile_modulatedlinear_kernel(
         load_unit(x_sb, x_rows, 0)
         load_unit(mod_sb, mod_rows, 2)
         load_unit(x_sb, x_rows, 1)
-        bias_rows = const.tile([P, FEATURES], BF16)
-        nc.vector.memset(bias_rows[:], 0.0)
-        nc.sync.dma_start(out=bias_rows[0:1, :], in_=bias.rearrange("(o n) -> o n", o=1))
+        bias_all = const.tile([P, FEATURES], BF16)
         for u in range(3, UNITS):
             load_unit(mod_sb, mod_rows, u)
             load_unit(x_sb, x_rows, u - 1)
+            if u == BIAS_LOAD_BEHIND:
+                nc.sync.dma_start(out=bias_all[:], in_=bias.partition_broadcast(P))
         load_unit(x_sb, x_rows, UNITS - 1)
 
         ident_f32 = const.tile([P, P], F32)
         make_identity(nc, ident_f32[:])
         ident_bf16 = const.tile([P, P], BF16)
         make_identity(nc, ident_bf16[:])
-        ones = const.tile([P, P], BF16)
-        nc.vector.memset(ones[:], 1.0)
         eps = const.tile([P, 1], F32)
         nc.vector.memset(eps[:], EPS)
         table_warmer = const.tile([P, 1], F32)
         nc.scalar.activation(out=table_warmer[:], in_=eps[:], func=ACT.Abs_reciprocal_sqrt)
 
         modb_col = const.tile([P, PACK], F32)
-        bias_all = const.tile([P, FEATURES], F32)
 
         def spread_mod_b():
             modb_t = psum.tile([P, P], BF16, tag="x_t", bufs=1)
             nc.tensor.transpose(modb_t[:], modb_rows[:], ident_bf16[:])
             nc.vector.tensor_copy(out=modb_col[:], in_=modb_t[:, 0:PACK])
-
-        def spread_bias():
-            bias_ps = psum.tile([P, FEATURES], F32, tag="x_t", bufs=1)
-            nc.tensor.matmul(out=bias_ps[:], lhsT=ones[:], rhs=bias_rows[:], start=True, stop=True)
-            nc.scalar.copy(out=bias_all[:], in_=bias_ps[:])
 
         w_grouped = const.tile([P, FEATURES, PACK], BF16, align_bytes=64)
         w2_grouped = const.tile([P, FEATURES, PACK], BF16, align_bytes=64)
@@ -122,7 +115,8 @@ def tile_modulatedlinear_kernel(
                         nc.tensor.transpose(
                             w_t[:, c, t, :], w_sb[:, 2 * half + c, t * P : (t + 1) * P], ident_bf16[:]
                         )
-                nc.scalar.copy(
+                copy = nc.scalar.copy if half == 0 else nc.vector.tensor_copy
+                copy(
                     out=w_grouped[:, 2 * half * P : 2 * (half + 1) * P, :].rearrange("p (c r) t -> p c r t", c=2),
                     in_=w_t[:].rearrange("p c t r -> p c r t"),
                 )
@@ -166,7 +160,7 @@ def tile_modulatedlinear_kernel(
 
         def group_modulation(u):
             mod_grouped = work.tile([P, UNIT, PACK], BF16, align_bytes=64)
-            copy = nc.vector.tensor_copy if u % 2 == 0 else nc.scalar.copy
+            copy = nc.scalar.copy if u % 2 == 0 else nc.vector.tensor_copy
             copy(
                 out=mod_grouped[:].bitcast(F32).rearrange("p (j r) h -> p j r h", j=UNIT_TILES),
                 in_=mod_t_of[u][:].rearrange("p j h r -> p j r h"),
@@ -294,7 +288,5 @@ def tile_modulatedlinear_kernel(
                 group_weight()
             if live(i - 1):
                 compute_s(i - 1)
-            if i == 1:
-                spread_bias()
             if live(i - 3):
                 demodulation(i - 3)

@@ -22,9 +22,8 @@ UNIT_TILES = 2
 UNIT = UNIT_TILES * P
 UNITS = TILES // UNIT_TILES
 STAGES = 5
-RESULT_BUFS = 8
+RING = 3
 VECTOR_BIAS_UNITS = 2
-BIAS_PIECES = 2
 XS = 0
 SS = 1
 RUN = 4
@@ -46,6 +45,7 @@ def tile_modulatedlinear_kernel(
         const = ctx.enter_context(tc.tile_pool(name="const", bufs=1))
         loads = ctx.enter_context(tc.tile_pool(name="loads", bufs=1))
         work = ctx.enter_context(tc.tile_pool(name="work", bufs=3))
+        ring = ctx.enter_context(tc.tile_pool(name="ring", bufs=1))
         psum = ctx.enter_context(tc.psum_pool(name="psum", bufs=2))
 
         mod_sb = [loads.tile([P, UNIT_TILES, K], BF16, name="mod_sb%d" % u) for u in range(UNITS)]
@@ -134,9 +134,21 @@ def tile_modulatedlinear_kernel(
                 in_=w2_grouped[:].rearrange("p o t -> p (o t)"),
             )
 
-        def quantise(grouped, words, what):
-            codes = work.tile([P, words], U32, align_bytes=64, name=what + "_codes")
-            scales = work.tile([P, words], U8, align_bytes=64, name=what + "_scales")
+        mod_bytes = UNIT * PACK * 2
+        products_bytes = 2 * UNIT * PACK * 2
+        slot_a = mod_bytes + products_bytes
+        slot_b = UNIT_TILES * FEATURES * 4
+        base_b = RING * slot_a
+
+        def place_a(i, inside):
+            return (i % RING) * slot_a + inside
+
+        def place_b(u, inside):
+            return base_b + (u % RING) * slot_b + inside
+
+        def quantise(grouped, words, what, u, codes_at, scales_at):
+            codes = ring.tile([P, words], U32, align_bytes=64, name="%s_codes%d" % (what, u), offset=codes_at)
+            scales = ring.tile([P, words], U8, align_bytes=64, name="%s_scales%d" % (what, u), offset=scales_at)
             nc.vector.quantize_mx(out=codes[:].bitcast(FP8X4), scales=scales[:], in_=grouped)
             return codes, scales
 
@@ -149,6 +161,7 @@ def tile_modulatedlinear_kernel(
         products_q = {}
         y_of = {}
         demod_of = {}
+        scaled_of = {}
 
         def transpose_modulation(u):
             words = mod_sb[u][:].bitcast(F32)
@@ -159,7 +172,7 @@ def tile_modulatedlinear_kernel(
             mod_t_of[u] = mod_t
 
         def group_modulation(u):
-            mod_grouped = work.tile([P, UNIT, PACK], BF16, align_bytes=64)
+            mod_grouped = ring.tile([P, UNIT, PACK], BF16, align_bytes=64, name="mod_grouped%d" % u, offset=place_a(u + 1, 0))
             copy = nc.scalar.copy if u % 2 == 0 else nc.vector.tensor_copy
             copy(
                 out=mod_grouped[:].bitcast(F32).rearrange("p (j r) h -> p j r h", j=UNIT_TILES),
@@ -203,7 +216,9 @@ def tile_modulatedlinear_kernel(
 
         def multiply(u):
             s_sb = s_of[u]
-            products = work.tile([P, 2, UNIT, PACK], BF16, align_bytes=64)
+            products = ring.tile(
+                [P, 2, UNIT, PACK], BF16, align_bytes=64, name="products%d" % u, offset=place_a(u + 3, mod_bytes)
+            )
             nc.vector.tensor_tensor(
                 out=products[:, XS].rearrange("p (c i) t -> p c t i", i=RUN),
                 in0=x_t_of[u][:].rearrange("p t (c i) -> p c t i", i=RUN),
@@ -247,19 +262,33 @@ def tile_modulatedlinear_kernel(
                 y_of[u, j] = y_ps
                 demod_of[u, j] = demod
 
+        def gpsimd_adds(u):
+            return 0 <= u < UNITS - VECTOR_BIAS_UNITS
+
         def finish(u):
-            for j in range(UNIT_TILES):
-                result = work.tile([P, FEATURES], F32, bufs=RESULT_BUFS)
-                nc.vector.tensor_tensor(out=result[:], in0=y_of[u, j][:], in1=demod_of[u, j][:], op=ALU.mult)
-                if u >= UNITS - VECTOR_BIAS_UNITS:
+            if gpsimd_adds(u):
+                scaled = ring.tile([P, UNIT_TILES, FEATURES], F32, align_bytes=64, name="scaled%d" % u, offset=place_b(u, 0))
+                for j in range(UNIT_TILES):
+                    nc.vector.tensor_tensor(out=scaled[:, j, :], in0=y_of[u, j][:], in1=demod_of[u, j][:], op=ALU.mult)
+                scaled_of[u] = scaled
+            else:
+                for j in range(UNIT_TILES):
+                    result = work.tile([P, FEATURES], F32, bufs=2 * UNIT_TILES)
+                    nc.vector.tensor_tensor(out=result[:], in0=y_of[u, j][:], in1=demod_of[u, j][:], op=ALU.mult)
                     nc.vector.tensor_tensor(out=result[:], in0=result[:], in1=bias_all[:], op=ALU.add)
-                else:
-                    for piece in range(BIAS_PIECES):
-                        cols = slice(piece * FEATURES // BIAS_PIECES, (piece + 1) * FEATURES // BIAS_PIECES)
-                        nc.gpsimd.tensor_tensor(
-                            out=result[:, cols], in0=result[:, cols], in1=bias_all[:, cols], op=ALU.add
-                        )
-                nc.sync.dma_start(out=out_rows[:, u * UNIT_TILES + j, :], in_=result[:])
+                    nc.sync.dma_start(out=out_rows[:, u * UNIT_TILES + j, :], in_=result[:])
+
+        def add_bias(u):
+            finished = ring.tile(
+                [P, UNIT_TILES, FEATURES], F32, align_bytes=64, name="finished%d" % u, offset=place_a(u + 5, mod_bytes // 2)
+            )
+            nc.gpsimd.tensor_tensor(
+                out=finished[:],
+                in0=scaled_of[u][:],
+                in1=bias_all[:].unsqueeze(1).to_broadcast([P, UNIT_TILES, FEATURES]),
+                op=ALU.add,
+            )
+            nc.sync.dma_start(out=out_rows[:, u * UNIT_TILES : (u + 1) * UNIT_TILES, :], in_=finished[:])
 
         def live(u):
             return 0 <= u < UNITS
@@ -270,11 +299,25 @@ def tile_modulatedlinear_kernel(
             if live(i - 2):
                 transpose_x(i - 2)
             if live(i - 1):
-                mod_q[i - 1] = quantise(mod_grouped_of[i - 1][:].rearrange("p r t -> p (r t)"), UNIT, "mod")
+                mod_q[i - 1] = quantise(
+                    mod_grouped_of[i - 1][:].rearrange("p r t -> p (r t)"),
+                    UNIT,
+                    "mod",
+                    i - 1,
+                    place_b(i, 2 * UNIT * 4),
+                    place_b(i, 3 * UNIT * 4 + 2 * UNIT),
+                )
             if live(i - 3):
                 products_q[i - 3] = quantise(
-                    products_of[i - 3][:].rearrange("p a r t -> p (a r t)"), 2 * UNIT, "products"
+                    products_of[i - 3][:].rearrange("p a r t -> p (a r t)"),
+                    2 * UNIT,
+                    "products",
+                    i - 3,
+                    place_b(i, 0),
+                    place_b(i, 3 * UNIT * 4),
                 )
+            if gpsimd_adds(i - 5):
+                add_bias(i - 5)
             if i == 2:
                 quantise_weight()
             if live(i - 4):

@@ -83,11 +83,16 @@ def tile_modulatedlinear_kernel(
             if u == BIAS_LOAD_BEHIND:
                 nc.sync.dma_start(out=bias_all[:], in_=bias.partition_broadcast(P))
         load_unit(x_sb, x_rows, UNITS - 1)
+        bias_rows = const.tile([P, FEATURES], BF16)
+        nc.vector.memset(bias_rows[:], 0.0)
+        nc.sync.dma_start(out=bias_rows[0:1, :], in_=bias.rearrange("(o n) -> o n", o=1))
 
         ident_f32 = const.tile([P, P], F32)
         make_identity(nc, ident_f32[:])
         ident_bf16 = const.tile([P, P], BF16)
         make_identity(nc, ident_bf16[:])
+        ones = const.tile([P, P], BF16)
+        nc.vector.memset(ones[:], 1.0)
         eps = const.tile([P, 1], F32)
         nc.vector.memset(eps[:], EPS)
         table_warmer = const.tile([P, 1], F32)
@@ -262,6 +267,13 @@ def tile_modulatedlinear_kernel(
                 y_of[u, j] = y_ps
                 demod_of[u, j] = demod
 
+        bias_bank = []
+
+        def spread_bias():
+            bias_ps = psum.tile([P, FEATURES], F32, tag="mod_t", bufs=1)
+            nc.tensor.matmul(out=bias_ps[:], lhsT=ones[:], rhs=bias_rows[:], start=True, stop=True)
+            bias_bank.append(bias_ps)
+
         def gpsimd_adds(u):
             return 0 <= u < UNITS - VECTOR_BIAS_UNITS
 
@@ -275,7 +287,7 @@ def tile_modulatedlinear_kernel(
                 for j in range(UNIT_TILES):
                     result = work.tile([P, FEATURES], F32, bufs=2 * UNIT_TILES)
                     nc.vector.tensor_tensor(out=result[:], in0=y_of[u, j][:], in1=demod_of[u, j][:], op=ALU.mult)
-                    nc.vector.tensor_tensor(out=result[:], in0=result[:], in1=bias_all[:], op=ALU.add)
+                    nc.vector.tensor_tensor(out=result[:], in0=result[:], in1=bias_bank[0][:], op=ALU.add)
                     nc.sync.dma_start(out=out_rows[:, u * UNIT_TILES + j, :], in_=result[:])
 
         def add_bias(u):
@@ -331,5 +343,7 @@ def tile_modulatedlinear_kernel(
                 group_weight()
             if live(i - 1):
                 compute_s(i - 1)
+            if i == UNITS:
+                spread_bias()
             if live(i - 3):
                 demodulation(i - 3)

@@ -142,18 +142,13 @@ def tile_modulatedlinear_kernel(
         mod_bytes = UNIT * PACK * 2
         products_bytes = 2 * UNIT * PACK * 2
         slot_a = mod_bytes + products_bytes
-        slot_b = UNIT_TILES * FEATURES * 4
-        base_b = RING * slot_a
 
         def place_a(i, inside):
             return (i % RING) * slot_a + inside
 
-        def place_b(u, inside):
-            return base_b + (u % RING) * slot_b + inside
-
-        def quantise(grouped, words, what, u, codes_at, scales_at):
-            codes = ring.tile([P, words], U32, align_bytes=64, name="%s_codes%d" % (what, u), offset=codes_at)
-            scales = ring.tile([P, words], U8, align_bytes=64, name="%s_scales%d" % (what, u), offset=scales_at)
+        def quantise(grouped, words, what):
+            codes = work.tile([P, words], U32, align_bytes=64, name=what + "_codes")
+            scales = work.tile([P, words], U8, align_bytes=64, name=what + "_scales")
             nc.vector.quantize_mx(out=codes[:].bitcast(FP8X4), scales=scales[:], in_=grouped)
             return codes, scales
 
@@ -279,7 +274,7 @@ def tile_modulatedlinear_kernel(
 
         def finish(u):
             if gpsimd_adds(u):
-                scaled = ring.tile([P, UNIT_TILES, FEATURES], F32, align_bytes=64, name="scaled%d" % u, offset=place_b(u, 0))
+                scaled = work.tile([P, UNIT_TILES, FEATURES], F32)
                 for j in range(UNIT_TILES):
                     nc.vector.tensor_tensor(out=scaled[:, j, :], in0=y_of[u, j][:], in1=demod_of[u, j][:], op=ALU.mult)
                 scaled_of[u] = scaled
@@ -311,22 +306,10 @@ def tile_modulatedlinear_kernel(
             if live(i - 2):
                 transpose_x(i - 2)
             if live(i - 1):
-                mod_q[i - 1] = quantise(
-                    mod_grouped_of[i - 1][:].rearrange("p r t -> p (r t)"),
-                    UNIT,
-                    "mod",
-                    i - 1,
-                    place_b(i, 2 * UNIT * 4),
-                    place_b(i, 3 * UNIT * 4 + 2 * UNIT),
-                )
+                mod_q[i - 1] = quantise(mod_grouped_of[i - 1][:].rearrange("p r t -> p (r t)"), UNIT, "mod")
             if live(i - 3):
                 products_q[i - 3] = quantise(
-                    products_of[i - 3][:].rearrange("p a r t -> p (a r t)"),
-                    2 * UNIT,
-                    "products",
-                    i - 3,
-                    place_b(i, 0),
-                    place_b(i, 3 * UNIT * 4),
+                    products_of[i - 3][:].rearrange("p a r t -> p (a r t)"), 2 * UNIT, "products"
                 )
             if gpsimd_adds(i - 5):
                 add_bias(i - 5)

from contextlib import ExitStack

import concourse.mybir as mybir
from concourse.masks import make_identity

F32 = mybir.dt.float32
BF16 = mybir.dt.bfloat16
I32 = mybir.dt.int32
U32 = mybir.dt.uint32
U8 = mybir.dt.uint8
FP8X4 = mybir.dt.float8_e4m3fn_x4
ACT = mybir.ActivationFunctionType
ALU = mybir.AluOpType

P = 128
PACK = 4
K = P * PACK
FEATURES = 512
TOKENS = 4 * 512
TILES = TOKENS // P
UNIT_TILES = 2
UNIT = UNIT_TILES * P
UNITS = TILES // UNIT_TILES
STAGES = 5
RING = 3
VECTOR_BIAS_UNITS = 2
XS = 0
SS = 1
RUN = 4
BIAS_LOAD_BEHIND = 4
EPS = 1e-8

FLOPS = 3 * 2 * TOKENS * K * FEATURES


def tile_modulatedlinear_kernel(
    tc, x, modulation, weight, bias, mod_w_words, mod_w_scales, mod_b, out
):
    nc = tc.nc
    x_rows = x.flatten_outer_dims().rearrange("(p j) k -> p j k", j=TILES)
    mod_rows = modulation.flatten_outer_dims().rearrange("(p j) k -> p j k", j=TILES)
    out_rows = out.flatten_outer_dims().rearrange("(p j) n -> p j n", j=TILES)

    with ExitStack() as ctx:
        const = ctx.enter_context(tc.tile_pool(name="const", bufs=1))
        loads = ctx.enter_context(tc.tile_pool(name="loads", bufs=1))
        work = ctx.enter_context(tc.tile_pool(name="work", bufs=3))
        ring = ctx.enter_context(tc.tile_pool(name="ring", bufs=1))
        psum = ctx.enter_context(tc.psum_pool(name="psum", bufs=2))

        mod_sb = [loads.tile([P, UNIT_TILES, K], BF16, name="mod_sb%d" % u) for u in range(UNITS)]
        x_sb = [loads.tile([P, UNIT_TILES, K], BF16, name="x_sb%d" % u) for u in range(UNITS)]

        def load_unit(tiles, rows, u):
            nc.sync.dma_start(out=tiles[u][:], in_=rows[:, u * UNIT_TILES : (u + 1) * UNIT_TILES, :])

        load_unit(mod_sb, mod_rows, 0)
        w_sb = loads.tile([P, PACK, K], BF16)
        nc.sync.dma_start(out=w_sb[:], in_=weight.rearrange("(c p) k -> p c k", p=P))
        w1_scales = const.tile([P, FEATURES], U8, align_bytes=64)
        nc.vector.memset(w1_scales[:].bitcast(I32), 0)
        for quadrant in range(4):
            nc.sync.dma_start(
                out=w1_scales[32 * quadrant : 32 * quadrant + 4, :].bitcast(I32),
                in_=mod_w_scales[0, 4 * quadrant : 4 * quadrant + 4, :].bitcast(I32),
            )
        w1_codes = const.tile([P, FEATURES], U32, align_bytes=64)
        nc.sync.dma_start(
            out=w1_codes[:].bitcast(I32),
            in_=mod_w_words[0].rearrange("p n t -> p (n t)").bitcast(I32),
        )
        modb_rows = const.tile([P, P], BF16)
        nc.vector.memset(modb_rows[:], 0.0)
        nc.sync.dma_start(out=modb_rows[0:PACK, :], in_=mod_b.rearrange("(t p) -> t p", p=P))
        load_unit(mod_sb, mod_rows, 1)
        load_unit(x_sb, x_rows, 0)
        load_unit(mod_sb, mod_rows, 2)
        load_unit(x_sb, x_rows, 1)
        bias_all = const.tile([P, FEATURES], BF16)
        for u in range(3, UNITS):
            load_unit(mod_sb, mod_rows, u)
            load_unit(x_sb, x_rows, u - 1)
            if u == BIAS_LOAD_BEHIND:
                nc.sync.dma_start(out=bias_all[:], in_=bias.partition_broadcast(P))
        load_unit(x_sb, x_rows, UNITS - 1)
        bias_rows = const.tile([P, FEATURES], BF16)
        nc.vector.memset(bias_rows[:], 0.0)
        nc.sync.dma_start(out=bias_rows[0:1, :], in_=bias.rearrange("(o n) -> o n", o=1))

        ident_f32 = const.tile([P, P], F32)
        make_identity(nc, ident_f32[:])
        ident_bf16 = const.tile([P, P], BF16)
        make_identity(nc, ident_bf16[:])
        ones = const.tile([P, P], BF16)
        nc.vector.memset(ones[:], 1.0)
        eps = const.tile([P, 1], F32)
        nc.vector.memset(eps[:], EPS)
        table_warmer = const.tile([P, 1], F32)
        nc.scalar.activation(out=table_warmer[:], in_=eps[:], func=ACT.Abs_reciprocal_sqrt)

        modb_col = const.tile([P, PACK], F32)

        def spread_mod_b():
            modb_t = psum.tile([P, P], BF16, tag="x_t", bufs=1)
            nc.tensor.transpose(modb_t[:], modb_rows[:], ident_bf16[:])
            nc.vector.tensor_copy(out=modb_col[:], in_=modb_t[:, 0:PACK])

        w_grouped = const.tile([P, FEATURES, PACK], BF16, align_bytes=64)
        w2_grouped = const.tile([P, FEATURES, PACK], BF16, align_bytes=64)
        w_codes = const.tile([P, FEATURES], U32, align_bytes=64)
        w_scales = const.tile([P, FEATURES], U8, align_bytes=64)
        w2_codes = const.tile([P, FEATURES], U32, align_bytes=64)
        w2_scales = const.tile([P, FEATURES], U8, align_bytes=64)

        def group_weight():
            for half, tag in enumerate(("q", "y")):
                w_t = psum.tile([P, 2, PACK, P], BF16, tag=tag, name="w_t")
                for c in range(2):
                    for t in range(PACK):
                        nc.tensor.transpose(
                            w_t[:, c, t, :], w_sb[:, 2 * half + c, t * P : (t + 1) * P], ident_bf16[:]
                        )
                copy = nc.scalar.copy if half == 0 else nc.vector.tensor_copy
                copy(
                    out=w_grouped[:, 2 * half * P : 2 * (half + 1) * P, :].rearrange("p (c r) t -> p c r t", c=2),
                    in_=w_t[:].rearrange("p c t r -> p c r t"),
                )

        def quantise_weight():
            nc.vector.tensor_tensor(out=w2_grouped[:], in0=w_grouped[:], in1=w_grouped[:], op=ALU.mult)
            nc.vector.quantize_mx(
                out=w_codes[:].bitcast(FP8X4),
                scales=w_scales[:],
                in_=w_grouped[:].rearrange("p o t -> p (o t)"),
            )
            nc.vector.quantize_mx(
                out=w2_codes[:].bitcast(FP8X4),
                scales=w2_scales[:],
                in_=w2_grouped[:].rearrange("p o t -> p (o t)"),
            )

        mod_bytes = UNIT * PACK * 2
        products_bytes = 2 * UNIT * PACK * 2
        slot_a = mod_bytes + products_bytes

        def place_a(i, inside):
            return (i % RING) * slot_a + inside

        def quantise(grouped, words, what):
            codes = work.tile([P, words], U32, align_bytes=64, name=what + "_codes")
            scales = work.tile([P, words], U8, align_bytes=64, name=what + "_scales")
            nc.vector.quantize_mx(out=codes[:].bitcast(FP8X4), scales=scales[:], in_=grouped)
            return codes, scales

        mod_t_of = {}
        mod_grouped_of = {}
        mod_q = {}
        s_of = {}
        x_t_of = {}
        products_of = {}
        products_q = {}
        y_of = {}
        demod_of = {}
        scaled_of = {}

        def transpose_modulation(u):
            words = mod_sb[u][:].bitcast(F32)
            mod_t = psum.tile([P, UNIT_TILES, 2, P], F32, tag="mod_t", bufs=1)
            for j in range(UNIT_TILES):
                for h in range(2):
                    nc.tensor.transpose(mod_t[:, j, h, :], words[:, j, h : K // 2 : 2], ident_f32[:])
            mod_t_of[u] = mod_t

        def group_modulation(u):
            mod_grouped = ring.tile([P, UNIT, PACK], BF16, align_bytes=64, name="mod_grouped%d" % u, offset=place_a(u + 1, 0))
            copy = nc.scalar.copy if u % 2 == 0 else nc.vector.tensor_copy
            copy(
                out=mod_grouped[:].bitcast(F32).rearrange("p (j r) h -> p j r h", j=UNIT_TILES),
                in_=mod_t_of[u][:].rearrange("p j h r -> p j r h"),
            )
            mod_grouped_of[u] = mod_grouped

        def compute_s(u):
            codes, scales = mod_q[u]
            s_sb = work.tile([P, PACK, UNIT], F32)
            for pair in range(PACK // 2):
                s_ps = psum.tile([P, 2, UNIT], F32, tag="s")
                for t in (2 * pair, 2 * pair + 1):
                    nc.tensor.matmul_mx(
                        out=s_ps[:, t % 2, :],
                        lhsT=w1_codes[:, t * P : (t + 1) * P].bitcast(FP8X4),
                        lhsT_scale=w1_scales[:, t * P : (t + 1) * P],
                        rhs=codes[:].bitcast(FP8X4),
                        rhs_scale=scales[:],
                        start=True,
                        stop=True,
                    )
                for t in (2 * pair + 1, 2 * pair):
                    nc.scalar.activation(
                        out=s_sb[:, t, :],
                        in_=s_ps[:, t % 2, :],
                        func=ACT.Identity,
                        bias=modb_col[:, t : t + 1],
                        scale=1.0,
                    )
            s_of[u] = s_sb

        def transpose_x(u):
            x_t = psum.tile([P, PACK, UNIT], BF16, tag="x_t", bufs=1)
            for j in range(UNIT_TILES):
                for t in range(PACK):
                    nc.tensor.transpose(
                        x_t[:, t, j * P : (j + 1) * P], x_sb[u][:, j, t * P : (t + 1) * P], ident_bf16[:]
                    )
            x_t_of[u] = x_t

        def multiply(u):
            s_sb = s_of[u]
            products = ring.tile(
                [P, 2, UNIT, PACK], BF16, align_bytes=64, name="products%d" % u, offset=place_a(u + 3, mod_bytes)
            )
            nc.vector.tensor_tensor(
                out=products[:, XS].rearrange("p (c i) t -> p c t i", i=RUN),
                in0=x_t_of[u][:].rearrange("p t (c i) -> p c t i", i=RUN),
                in1=s_sb[:].rearrange("p t (c i) -> p c t i", i=RUN),
                op=ALU.mult,
            )
            nc.scalar.activation(
                out=products[:, SS].rearrange("p (c i) t -> p c t i", i=RUN), in_=s_sb[:].rearrange("p t (c i) -> p c t i", i=RUN), func=ACT.Square
            )
            products_of[u] = products

        def demodulation(u):
            codes, scales = products_q[u]
            for j in range(UNIT_TILES):
                xs_cols = slice(XS * UNIT + j * P, XS * UNIT + (j + 1) * P)
                ss_cols = slice(SS * UNIT + j * P, SS * UNIT + (j + 1) * P)
                q_ps = psum.tile([P, FEATURES], F32, tag="q")
                nc.tensor.matmul_mx(
                    out=q_ps[:],
                    lhsT=codes[:, ss_cols].bitcast(FP8X4),
                    lhsT_scale=scales[:, ss_cols],
                    rhs=w2_codes[:].bitcast(FP8X4),
                    rhs_scale=w2_scales[:],
                    start=True,
                    stop=True,
                )
                y_ps = psum.tile([P, FEATURES], F32, tag="y")
                nc.tensor.matmul_mx(
                    out=y_ps[:],
                    lhsT=codes[:, xs_cols].bitcast(FP8X4),
                    lhsT_scale=scales[:, xs_cols],
                    rhs=w_codes[:].bitcast(FP8X4),
                    rhs_scale=w_scales[:],
                    start=True,
                    stop=True,
                )
                demod = work.tile([P, FEATURES], F32, bufs=2 * UNIT_TILES)
                nc.scalar.activation(
                    out=demod[:], in_=q_ps[:], func=ACT.Abs_reciprocal_sqrt, bias=EPS, scale=1.0
                )
                y_of[u, j] = y_ps
                demod_of[u, j] = demod

        bias_bank = []

        def spread_bias():
            bias_ps = psum.tile([P, FEATURES], F32, tag="mod_t", bufs=1)
            nc.tensor.matmul(out=bias_ps[:], lhsT=ones[:], rhs=bias_rows[:], start=True, stop=True)
            bias_bank.append(bias_ps)

        def gpsimd_adds(u):
            return 0 <= u < UNITS - VECTOR_BIAS_UNITS

        def finish(u):
            if gpsimd_adds(u):
                scaled = work.tile([P, UNIT_TILES, FEATURES], F32)
                for j in range(UNIT_TILES):
                    nc.vector.tensor_tensor(out=scaled[:, j, :], in0=y_of[u, j][:], in1=demod_of[u, j][:], op=ALU.mult)
                scaled_of[u] = scaled
            else:
                for j in range(UNIT_TILES):
                    result = work.tile([P, FEATURES], F32, bufs=2 * UNIT_TILES)
                    nc.vector.tensor_tensor(out=result[:], in0=y_of[u, j][:], in1=demod_of[u, j][:], op=ALU.mult)
                    nc.vector.tensor_tensor(out=result[:], in0=result[:], in1=bias_bank[0][:], op=ALU.add)
                    nc.sync.dma_start(out=out_rows[:, u * UNIT_TILES + j, :], in_=result[:])

        def add_bias(u):
            finished = ring.tile(
                [P, UNIT_TILES, FEATURES], F32, align_bytes=64, name="finished%d" % u, offset=place_a(u + 5, mod_bytes // 2)
            )
            nc.gpsimd.tensor_tensor(
                out=finished[:],
                in0=scaled_of[u][:],
                in1=bias_all[:].unsqueeze(1).to_broadcast([P, UNIT_TILES, FEATURES]),
                op=ALU.add,
            )
            nc.sync.dma_start(out=out_rows[:, u * UNIT_TILES : (u + 1) * UNIT_TILES, :], in_=finished[:])

        def live(u):
            return 0 <= u < UNITS

        for i in range(UNITS + STAGES - 1):
            if live(i):
                transpose_modulation(i)
            if live(i - 2):
                transpose_x(i - 2)
            if live(i - 1):
                mod_q[i - 1] = quantise(mod_grouped_of[i - 1][:].rearrange("p r t -> p (r t)"), UNIT, "mod")
            if live(i - 3):
                products_q[i - 3] = quantise(
                    products_of[i - 3][:].rearrange("p a r t -> p (a r t)"), 2 * UNIT, "products"
                )
            if gpsimd_adds(i - 5):
                add_bias(i - 5)
            if i == 2:
                quantise_weight()
            if live(i - 4):
                finish(i - 4)
            if live(i - 2):
                multiply(i - 2)
            if live(i):
                group_modulation(i)
            if i == 0:
                spread_mod_b()
                group_weight()
            if live(i - 1):
                compute_s(i - 1)
            if i == UNITS:
                spread_bias()
            if live(i - 3):
                demodulation(i - 3)
